import numpy as np
import ml_dtypes


def mxq(x, axis, fmt="e4m3"):
    dtype, down = {"e4m3": (ml_dtypes.float8_e4m3fn, 7), "e5m2": (ml_dtypes.float8_e5m2, 14)}[fmt]
    v = np.moveaxis(np.asarray(x, np.float32).astype(ml_dtypes.bfloat16).astype(np.float64), axis, -1)
    blocks = v.reshape(v.shape[:-1] + (-1, 32))
    amax = np.abs(blocks).max(-1, keepdims=True)
    byte = np.maximum(np.where(amax > 0, np.frexp(amax)[1] - 1 + 127, 0) - down, 1)
    scale = np.exp2(byte - 127.0)
    codes = (blocks / scale).astype(np.float32).astype(dtype).astype(np.float64)
    return np.moveaxis((codes * scale).reshape(v.shape), -1, axis)


WIDE = False


def mx_kscale(k):
    if not WIDE:
        return np.ones(k)
    levels = np.array([10, -10, 5, -5, 0])
    a = np.random.permutation(np.resize(levels, k // 512 * 4)).reshape(k // 512, 4)
    idx = np.arange(k)
    return np.exp2(a[idx // 512, idx % 128 // 32])


BF16 = ml_dtypes.bfloat16


def bf(x):
    return np.asarray(x, np.float32).astype(BF16)


def f64(x):
    return np.asarray(x).astype(np.float64)


E2M1 = np.array([0.0, 0.5, 1.0, 1.5, 2.0, 3.0, 4.0, 6.0, -0.0, -0.5, -1.0, -1.5, -2.0, -3.0, -4.0, -6.0])


def pack_weight(w, fmt):
    k, n = w.shape
    w = f64(bf(w)).reshape(k // 32, 32, n)
    amax = np.abs(w).max(1)
    if fmt == "e4m3":
        byte = np.frexp(amax)[1] - 1 + 127 - 7
    else:
        mant, ex = np.frexp(amax / 6.0)
        byte = np.where(mant > 0.5, ex, ex - 1) + 127
    byte = np.clip(np.where(amax > 0, byte, 1), 1, 254)
    scaled = (w * np.exp2(127.0 - byte)[:, None, :]).reshape(k, n).astype(np.float32)
    by_word = np.ascontiguousarray(scaled.reshape(k // 512, 128, 4, n).transpose(0, 1, 3, 2))
    if fmt == "e4m3":
        words = by_word.astype(ml_dtypes.float8_e4m3fn).view(np.uint8)
    else:
        c = by_word.astype(ml_dtypes.float4_e2m1fn).view(np.uint8) & 0xF
        words = c[..., 0::2] | (c[..., 1::2] << 4)
    return np.ascontiguousarray(words), np.ascontiguousarray(byte.astype(np.uint8).reshape(k // 512, 16, n))


def unpack_weight(words, scales, fmt):
    g, p, n, _ = words.shape
    if fmt == "e4m3":
        vals = np.ascontiguousarray(words).view(ml_dtypes.float8_e4m3fn).astype(np.float64)
    else:
        nib = np.empty((g, p, n, 4), np.uint8)
        nib[..., 0::2] = words & 0xF
        nib[..., 1::2] = words >> 4
        vals = E2M1[nib]
    vals = vals * np.repeat(np.exp2(scales.astype(np.float64) - 127.0), 8, axis=1)[..., None]
    return vals.transpose(0, 1, 3, 2).reshape(g * 512, n)

def pack4(w):
    words, scales = pack_weight(w, "e2m1")
    return words.reshape(words.shape[0], 128, -1), scales


def unpack4(words, scales):
    return unpack_weight(words.reshape(words.shape[0], 128, -1, 2), scales, "e2m1")


N1, N2, N3, R1, R = 16, 16, 512, 512, 8192


def setup_inputs():
    s = mx_kscale(R)
    g = R ** (-1.0 / 6.0)
    X = bf(np.random.standard_normal((N1, N2, N3)))
    A = bf(np.random.standard_normal((N1, R)) * g * s)
    B = bf(np.random.standard_normal((N2, R)) * g)
    c = np.random.standard_normal((N3, R)) * g / s
    words, scales = pack4(np.ascontiguousarray(c.T))
    return {"X": X, "A": A, "B": B, "C_words": words, "C_scales": scales}


def reference(X, A, B, C_words, C_scales):
    p = (f64(A)[:, None, :] * f64(B)[None, :, :]).reshape(N1 * N2, R)
    approx = mxq(p, 1, "e4m3") @ unpack4(C_words, C_scales)
    return approx.reshape(N1, N2, N3) - f64(X)

@@ -1,0 +1,145 @@
+from contextlib import ExitStack
+
+import concourse.mybir as mybir
+from concourse.masks import make_identity
+
+F32 = mybir.dt.float32
+BF16 = mybir.dt.bfloat16
+U8 = mybir.dt.uint8
+U32 = mybir.dt.uint32
+I32 = mybir.dt.int32
+FP8X4 = mybir.dt.float8_e4m3fn_x4
+FP4X4 = mybir.dt.float4_e2m1fn_x4
+
+N1, N2, N3, R = 16, 16, 512, 8192
+P = 128
+PACK = 4
+K_PASS = P * PACK
+PASSES = R // K_PASS
+HALF = P // PASSES
+M_TILES = N1 // HALF
+GROUP = 2
+LOAD_PASSES = 4
+QUADRANTS = 4
+
+FLOPS = 2 * N1 * N2 * N3 * R
+
+
+def tile_recon_loss_pa_kernel(tc, X, A, B, C_words, C_scales, out):
+    nc = tc.nc
+    with ExitStack() as ctx:
+        keep = ctx.enter_context(tc.tile_pool(name="keep", bufs=1))
+        psum = ctx.enter_context(tc.psum_pool(name="psum", bufs=1))
+        ctx.enter_context(tc.manual_schedule())
+
+        def load_half(rows, name):
+            raw = keep.tile([P, K_PASS], BF16, name=name)
+            nc.sync.dma_start(out=raw[:], in_=rows.rearrange("i (g r) -> g i r", r=K_PASS))
+            return raw
+
+        a_raw0 = load_half(A[0:HALF, :], "a_raw0")
+        b_raw0 = load_half(B[0:HALF, :], "b_raw0")
+        b_raw1 = load_half(B[HALF : 2 * HALF, :], "b_raw1")
+        a_raw1 = load_half(A[HALF : 2 * HALF, :], "a_raw1")
+
+        ident = keep.tile([P, P], F32, name="ident")
+        make_identity(nc, ident[:])
+
+        w_scales = keep.tile([P, PASSES, N3], U8, name="w_scales", align_bytes=64)
+        nc.vector.memset(w_scales[:].bitcast(I32), 0)
+        scale_rows = C_scales.bitcast(I32)
+        for quad in range(QUADRANTS):
+            nc.sync.dma_start(
+                out=w_scales[32 * quad : 32 * quad + 4, :, :].bitcast(I32),
+                in_=scale_rows[:, 4 * quad : 4 * quad + 4, :].rearrange("g q n -> q g n"),
+            )
+
+        w_words = keep.tile([P, PASSES, 2 * N3], U8, name="w_words", align_bytes=64)
+        word_rows = C_words.bitcast(I32).rearrange("g p w -> p g w")
+        for g0 in range(0, PASSES, LOAD_PASSES):
+            nc.sync.dma_start(
+                out=w_words[:, g0 : g0 + LOAD_PASSES, :].bitcast(I32),
+                in_=word_rows[:, g0 : g0 + LOAD_PASSES, :],
+            )
+
+        x_rows = X.rearrange("i j n -> (i j) n")
+        out_rows = out.rearrange("i j n -> (i j) n")
+        x_sb = []
+        for m in range(M_TILES):
+            x_tile = keep.tile([P, N3], BF16, name="x_sb%d" % m)
+            nc.sync.dma_start(out=x_tile[:], in_=x_rows[m * P : (m + 1) * P, :])
+            x_sb.append(x_tile)
+
+        a_t = [keep.tile([P, PASSES, HALF, PACK], BF16, name="a_t%d" % m) for m in range(M_TILES)]
+        b_t = keep.tile([P, PASSES, N2, PACK], BF16, name="b_t")
+
+        def turn_half(raw, name):
+            words = raw[:].bitcast(F32)
+            turned = psum.tile([P, 2, P], F32, name=name)
+            for u in range(2):
+                nc.tensor.transpose(turned[:, u, :], words[:, u : K_PASS // 2 : 2], ident[:])
+            return turned[:].rearrange("p u (g i) -> p g i u", i=HALF)
+
+        a_ps0 = turn_half(a_raw0, "a_ps0")
+        nc.vector.tensor_copy(out=a_t[0][:].bitcast(F32), in_=a_ps0)
+        b_ps0 = turn_half(b_raw0, "b_ps0")
+        nc.scalar.copy(out=b_t[:, :, 0:HALF, :].bitcast(F32), in_=b_ps0)
+        b_ps1 = turn_half(b_raw1, "b_ps1")
+        nc.vector.tensor_copy(out=b_t[:, :, HALF : 2 * HALF, :].bitcast(F32), in_=b_ps1)
+        a_ps1 = turn_half(a_raw1, "a_ps1")
+        nc.scalar.copy(out=a_t[1][:].bitcast(F32), in_=a_ps1)
+
+        prod = [
+            keep.tile([P, PASSES, HALF, N2, PACK], BF16, name="prod%d" % m, align_bytes=64)
+            for m in range(M_TILES)
+        ]
+        codes = [keep.tile([P, PASSES, P], U32, name="codes%d" % m, align_bytes=64) for m in range(M_TILES)]
+        code_scales = [
+            keep.tile([P, PASSES, P], U8, name="code_scales%d" % m, align_bytes=64) for m in range(M_TILES)
+        ]
+        acc = [psum.tile([P, N3], F32, name="acc%d" % m) for m in range(M_TILES)]
+
+        def multiply(m, g0):
+            shape = [P, GROUP, HALF, N2, PACK]
+            nc.vector.tensor_tensor(
+                out=prod[m][:, g0 : g0 + GROUP, :, :, :],
+                in0=a_t[m][:, g0 : g0 + GROUP, :, :].unsqueeze(3).to_broadcast(shape),
+                in1=b_t[:, g0 : g0 + GROUP, :, :].unsqueeze(2).to_broadcast(shape),
+                op=mybir.AluOpType.mult,
+            )
+
+        def quantise(m, g0):
+            nc.vector.quantize_mx(
+                out=codes[m][:, g0 : g0 + GROUP, :].rearrange("p g c -> p (g c)").bitcast(FP8X4),
+                scales=code_scales[m][:, g0 : g0 + GROUP, :].rearrange("p g c -> p (g c)"),
+                in_=prod[m][:, g0 : g0 + GROUP, :, :, :].rearrange("p g i j t -> p (g i j t)"),
+            )
+
+        def contract(m, g0):
+            for g in range(g0, g0 + GROUP):
+                nc.tensor.matmul_mx(
+                    out=acc[m][:],
+                    lhsT=codes[m][:, g, :].bitcast(FP8X4),
+                    lhsT_scale=code_scales[m][:, g, :],
+                    rhs=w_words[:, g, :].bitcast(FP4X4),
+                    rhs_scale=w_scales[:, g, :],
+                    start=(g == 0),
+                    stop=(g == PASSES - 1),
+                )
+
+        def finish(m):
+            result = keep.tile([P, N3], F32, name="result%d" % m)
+            nc.vector.tensor_tensor(
+                out=result[:], in0=acc[m][:], in1=x_sb[m][:], op=mybir.AluOpType.subtract
+            )
+            nc.sync.dma_start(out=out_rows[m * P : (m + 1) * P, :], in_=result[:])
+
+        steps = [(m, g0) for m in range(M_TILES) for g0 in range(0, PASSES, GROUP)]
+        for s in range(len(steps) + 2):
+            if s < len(steps):
+                multiply(*steps[s])
+            if 1 <= s <= len(steps):
+                quantise(*steps[s - 1])
+                contract(*steps[s - 1])
+            if s >= 2 and steps[s - 2][1] == PASSES - GROUP:
+                finish(steps[s - 2][0])

@@ -135,11 +135,11 @@ def tile_recon_loss_pa_kernel(tc, X, A, B, C_words, C_scales, out):
             nc.sync.dma_start(out=out_rows[m * P : (m + 1) * P, :], in_=result[:])
 
         steps = [(m, g0) for m in range(M_TILES) for g0 in range(0, PASSES, GROUP)]
-        for s in range(len(steps) + 2):
+        for s in range(len(steps) + 1):
             if s < len(steps):
                 multiply(*steps[s])
-            if 1 <= s <= len(steps):
+            if s >= 1:
                 quantise(*steps[s - 1])
                 contract(*steps[s - 1])
-            if s >= 2 and steps[s - 2][1] == PASSES - GROUP:
-                finish(steps[s - 2][0])
+        for m in range(M_TILES):
+            finish(m)

@@ -46,21 +46,18 @@ def tile_recon_loss_pa_kernel(tc, X, A, B, C_words, C_scales, out):
         make_identity(nc, ident[:])
 
         w_scales = keep.tile([P, PASSES, N3], U8, name="w_scales", align_bytes=64)
-        nc.vector.memset(w_scales[:].bitcast(I32), 0)
         scale_rows = C_scales.bitcast(I32)
-        for quad in range(QUADRANTS):
-            nc.sync.dma_start(
-                out=w_scales[32 * quad : 32 * quad + 4, :, :].bitcast(I32),
-                in_=scale_rows[:, 4 * quad : 4 * quad + 4, :].rearrange("g q n -> q g n"),
-            )
-
         w_words = keep.tile([P, PASSES, 2 * N3], U8, name="w_words", align_bytes=64)
         word_rows = C_words.bitcast(I32).rearrange("g p w -> p g w")
         for g0 in range(0, PASSES, LOAD_PASSES):
-            nc.sync.dma_start(
-                out=w_words[:, g0 : g0 + LOAD_PASSES, :].bitcast(I32),
-                in_=word_rows[:, g0 : g0 + LOAD_PASSES, :],
-            )
+            group = slice(g0, g0 + LOAD_PASSES)
+            nc.vector.memset(w_scales[:, group, :].bitcast(I32), 0)
+            for quad in range(QUADRANTS):
+                nc.sync.dma_start(
+                    out=w_scales[32 * quad : 32 * quad + 4, group, :].bitcast(I32),
+                    in_=scale_rows[group, 4 * quad : 4 * quad + 4, :].rearrange("g q n -> q g n"),
+                )
+            nc.sync.dma_start(out=w_words[:, group, :].bitcast(I32), in_=word_rows[:, group, :])
 
         x_rows = X.rearrange("i j n -> (i j) n")
         out_rows = out.rearrange("i j n -> (i j) n")

@@ -16,8 +16,10 @@ P = 128
 PACK = 4
 K_PASS = P * PACK
 PASSES = R // K_PASS
-HALF = P // PASSES
-M_TILES = N1 // HALF
+HALF_PASSES = P // N1
+HALVES = PASSES // HALF_PASSES
+J_TILE = P // N1
+M_TILES = N2 // J_TILE
 GROUP = 2
 LOAD_PASSES = 4
 QUADRANTS = 4
@@ -32,15 +34,17 @@ def tile_recon_loss_pa_kernel(tc, X, A, B, C_words, C_scales, out):
         psum = ctx.enter_context(tc.psum_pool(name="psum", bufs=1))
         ctx.enter_context(tc.manual_schedule())
 
-        def load_half(rows, name):
+        def load_half(factor, h, name):
             raw = keep.tile([P, K_PASS], BF16, name=name)
-            nc.sync.dma_start(out=raw[:], in_=rows.rearrange("i (g r) -> g i r", r=K_PASS))
+            columns = factor[:, h * HALF_PASSES * K_PASS : (h + 1) * HALF_PASSES * K_PASS]
+            nc.sync.dma_start(out=raw[:], in_=columns.rearrange("i (g r) -> i g r", r=K_PASS))
             return raw
 
-        a_raw0 = load_half(A[0:HALF, :], "a_raw0")
-        b_raw0 = load_half(B[0:HALF, :], "b_raw0")
-        b_raw1 = load_half(B[HALF : 2 * HALF, :], "b_raw1")
-        a_raw1 = load_half(A[HALF : 2 * HALF, :], "a_raw1")
+        a_raw = []
+        b_raw = []
+        for h in range(HALVES):
+            a_raw.append(load_half(A, h, "a_raw%d" % h))
+            b_raw.append(load_half(B, h, "b_raw%d" % h))
 
         ident = keep.tile([P, P], F32, name="ident")
         make_identity(nc, ident[:])
@@ -59,15 +63,13 @@ def tile_recon_loss_pa_kernel(tc, X, A, B, C_words, C_scales, out):
                 )
             nc.sync.dma_start(out=w_words[:, group, :].bitcast(I32), in_=word_rows[:, group, :])
 
-        x_rows = X.rearrange("i j n -> (i j) n")
-        out_rows = out.rearrange("i j n -> (i j) n")
         x_sb = []
         for m in range(M_TILES):
             x_tile = keep.tile([P, N3], BF16, name="x_sb%d" % m)
-            nc.sync.dma_start(out=x_tile[:], in_=x_rows[m * P : (m + 1) * P, :])
+            nc.sync.dma_start(out=x_tile[:], in_=X[:, m * J_TILE : (m + 1) * J_TILE, :])
             x_sb.append(x_tile)
 
-        a_t = [keep.tile([P, PASSES, HALF, PACK], BF16, name="a_t%d" % m) for m in range(M_TILES)]
+        a_t = keep.tile([P, PASSES, N1, PACK], BF16, name="a_t")
         b_t = keep.tile([P, PASSES, N2, PACK], BF16, name="b_t")
 
         def turn_half(raw, name):
@@ -75,19 +77,20 @@ def tile_recon_loss_pa_kernel(tc, X, A, B, C_words, C_scales, out):
             turned = psum.tile([P, 2, P], F32, name=name)
             for u in range(2):
                 nc.tensor.transpose(turned[:, u, :], words[:, u : K_PASS // 2 : 2], ident[:])
-            return turned[:].rearrange("p u (g i) -> p g i u", i=HALF)
+            return turned[:].rearrange("p u (i g) -> p g i u", g=HALF_PASSES)
 
-        a_ps0 = turn_half(a_raw0, "a_ps0")
-        nc.vector.tensor_copy(out=a_t[0][:].bitcast(F32), in_=a_ps0)
-        b_ps0 = turn_half(b_raw0, "b_ps0")
-        nc.scalar.copy(out=b_t[:, :, 0:HALF, :].bitcast(F32), in_=b_ps0)
-        b_ps1 = turn_half(b_raw1, "b_ps1")
-        nc.vector.tensor_copy(out=b_t[:, :, HALF : 2 * HALF, :].bitcast(F32), in_=b_ps1)
-        a_ps1 = turn_half(a_raw1, "a_ps1")
-        nc.scalar.copy(out=a_t[1][:].bitcast(F32), in_=a_ps1)
+        for h in range(HALVES):
+            passes = slice(h * HALF_PASSES, (h + 1) * HALF_PASSES)
+            a_turned = turn_half(a_raw[h], "a_turned%d" % h)
+            if h == 0:
+                nc.vector.tensor_copy(out=a_t[:, passes, :, :].bitcast(F32), in_=a_turned)
+            else:
+                nc.scalar.copy(out=a_t[:, passes, :, :].bitcast(F32), in_=a_turned)
+            b_turned = turn_half(b_raw[h], "b_turned%d" % h)
+            nc.scalar.copy(out=b_t[:, passes, :, :].bitcast(F32), in_=b_turned)
 
         prod = [
-            keep.tile([P, PASSES, HALF, N2, PACK], BF16, name="prod%d" % m, align_bytes=64)
+            keep.tile([P, PASSES, N1, J_TILE, PACK], BF16, name="prod%d" % m, align_bytes=64)
             for m in range(M_TILES)
         ]
         codes = [keep.tile([P, PASSES, P], U32, name="codes%d" % m, align_bytes=64) for m in range(M_TILES)]
@@ -97,11 +100,11 @@ def tile_recon_loss_pa_kernel(tc, X, A, B, C_words, C_scales, out):
         acc = [psum.tile([P, N3], F32, name="acc%d" % m) for m in range(M_TILES)]
 
         def multiply(m, g0):
-            shape = [P, GROUP, HALF, N2, PACK]
+            shape = [P, GROUP, N1, J_TILE, PACK]
             nc.vector.tensor_tensor(
                 out=prod[m][:, g0 : g0 + GROUP, :, :, :],
-                in0=a_t[m][:, g0 : g0 + GROUP, :, :].unsqueeze(3).to_broadcast(shape),
-                in1=b_t[:, g0 : g0 + GROUP, :, :].unsqueeze(2).to_broadcast(shape),
+                in0=a_t[:, g0 : g0 + GROUP, :, :].unsqueeze(3).to_broadcast(shape),
+                in1=b_t[:, g0 : g0 + GROUP, m * J_TILE : (m + 1) * J_TILE, :].unsqueeze(2).to_broadcast(shape),
                 op=mybir.AluOpType.mult,
             )
 
@@ -129,7 +132,7 @@ def tile_recon_loss_pa_kernel(tc, X, A, B, C_words, C_scales, out):
             nc.vector.tensor_tensor(
                 out=result[:], in0=acc[m][:], in1=x_sb[m][:], op=mybir.AluOpType.subtract
             )
-            nc.sync.dma_start(out=out_rows[m * P : (m + 1) * P, :], in_=result[:])
+            nc.sync.dma_start(out=out[:, m * J_TILE : (m + 1) * J_TILE, :], in_=result[:])
 
         steps = [(m, g0) for m in range(M_TILES) for g0 in range(0, PASSES, GROUP)]
         for s in range(len(steps) + 1):

@@ -16,11 +16,11 @@ P = 128
 PACK = 4
 K_PASS = P * PACK
 PASSES = R // K_PASS
-HALF_PASSES = P // N1
-HALVES = PASSES // HALF_PASSES
-J_TILE = P // N1
-M_TILES = N2 // J_TILE
-GROUP = 2
+ROWS = N1 + N2
+CHUNK = P // ROWS
+CHUNKS = PASSES // CHUNK
+I_TILE = P // N2
+M_TILES = N1 // I_TILE
 LOAD_PASSES = 4
 QUADRANTS = 4
 
@@ -34,17 +34,14 @@ def tile_recon_loss_pa_kernel(tc, X, A, B, C_words, C_scales, out):
         psum = ctx.enter_context(tc.psum_pool(name="psum", bufs=1))
         ctx.enter_context(tc.manual_schedule())
 
-        def load_half(factor, h, name):
-            raw = keep.tile([P, K_PASS], BF16, name=name)
-            columns = factor[:, h * HALF_PASSES * K_PASS : (h + 1) * HALF_PASSES * K_PASS]
-            nc.sync.dma_start(out=raw[:], in_=columns.rearrange("i (g r) -> i g r", r=K_PASS))
-            return raw
-
-        a_raw = []
-        b_raw = []
-        for h in range(HALVES):
-            a_raw.append(load_half(A, h, "a_raw%d" % h))
-            b_raw.append(load_half(B, h, "b_raw%d" % h))
+        raw = []
+        for c in range(CHUNKS):
+            tile = keep.tile([P, K_PASS], BF16, name="raw%d" % c)
+            columns = slice(c * CHUNK * K_PASS, (c + 1) * CHUNK * K_PASS)
+            half = P // 2
+            nc.sync.dma_start(out=tile[0:half, :], in_=A[:, columns].rearrange("i (g r) -> g i r", r=K_PASS))
+            nc.scalar.dma_start(out=tile[half:P, :], in_=B[:, columns].rearrange("j (g r) -> g j r", r=K_PASS))
+            raw.append(tile)
 
         ident = keep.tile([P, P], F32, name="ident")
         make_identity(nc, ident[:])
@@ -63,78 +60,71 @@ def tile_recon_loss_pa_kernel(tc, X, A, B, C_words, C_scales, out):
                 )
             nc.sync.dma_start(out=w_words[:, group, :].bitcast(I32), in_=word_rows[:, group, :])
 
-        x_sb = []
-        for m in range(M_TILES):
-            x_tile = keep.tile([P, N3], BF16, name="x_sb%d" % m)
-            nc.sync.dma_start(out=x_tile[:], in_=X[:, m * J_TILE : (m + 1) * J_TILE, :])
-            x_sb.append(x_tile)
+        x_sb = keep.tile([P, M_TILES, N3], BF16, name="x_sb")
+        nc.sync.dma_start(out=x_sb[:], in_=X.rearrange("(m i) j n -> (i j) m n", m=M_TILES))
 
-        a_t = keep.tile([P, PASSES, N1, PACK], BF16, name="a_t")
-        b_t = keep.tile([P, PASSES, N2, PACK], BF16, name="b_t")
-
-        def turn_half(raw, name):
-            words = raw[:].bitcast(F32)
-            turned = psum.tile([P, 2, P], F32, name=name)
+        ab = keep.tile([P, 2, PASSES, N1, PACK], BF16, name="ab")
+        for c in range(CHUNKS):
+            words = raw[c][:].bitcast(F32)
+            turned = psum.tile([P, 2, P], F32, name="turned%d" % c)
             for u in range(2):
                 nc.tensor.transpose(turned[:, u, :], words[:, u : K_PASS // 2 : 2], ident[:])
-            return turned[:].rearrange("p u (i g) -> p g i u", g=HALF_PASSES)
-
-        for h in range(HALVES):
-            passes = slice(h * HALF_PASSES, (h + 1) * HALF_PASSES)
-            a_turned = turn_half(a_raw[h], "a_turned%d" % h)
-            if h == 0:
-                nc.vector.tensor_copy(out=a_t[:, passes, :, :].bitcast(F32), in_=a_turned)
+            target = ab[:, :, c * CHUNK : (c + 1) * CHUNK, :, :].rearrange("p f g i t -> p f (g i t)").bitcast(F32)
+            target = target.rearrange("p f (q u) -> p f q u", u=2)
+            source = turned[:].rearrange("p u (f q) -> p f q u", f=2)
+            if c == 0:
+                nc.vector.tensor_copy(out=target, in_=source)
             else:
-                nc.scalar.copy(out=a_t[:, passes, :, :].bitcast(F32), in_=a_turned)
-            b_turned = turn_half(b_raw[h], "b_turned%d" % h)
-            nc.scalar.copy(out=b_t[:, passes, :, :].bitcast(F32), in_=b_turned)
+                nc.scalar.copy(out=target, in_=source)
 
-        prod = [
-            keep.tile([P, PASSES, N1, J_TILE, PACK], BF16, name="prod%d" % m, align_bytes=64)
-            for m in range(M_TILES)
-        ]
-        codes = [keep.tile([P, PASSES, P], U32, name="codes%d" % m, align_bytes=64) for m in range(M_TILES)]
-        code_scales = [
-            keep.tile([P, PASSES, P], U8, name="code_scales%d" % m, align_bytes=64) for m in range(M_TILES)
-        ]
+        prod = keep.tile([P, PASSES, N1, N2, PACK], BF16, name="prod", align_bytes=64)
+        codes = keep.tile([P, PASSES, N1 * N2], U32, name="codes", align_bytes=64)
+        code_scales = keep.tile([P, PASSES, N1 * N2], U8, name="code_scales", align_bytes=64)
         acc = [psum.tile([P, N3], F32, name="acc%d" % m) for m in range(M_TILES)]
 
-        def multiply(m, g0):
-            shape = [P, GROUP, N1, J_TILE, PACK]
+        def multiply(g, i):
+            shape = [P, g.stop - g.start, i.stop - i.start, N2, PACK]
             nc.vector.tensor_tensor(
-                out=prod[m][:, g0 : g0 + GROUP, :, :, :],
-                in0=a_t[:, g0 : g0 + GROUP, :, :].unsqueeze(3).to_broadcast(shape),
-                in1=b_t[:, g0 : g0 + GROUP, m * J_TILE : (m + 1) * J_TILE, :].unsqueeze(2).to_broadcast(shape),
+                out=prod[:, g, i, :, :],
+                in0=ab[:, 0, g, i, :].unsqueeze(3).to_broadcast(shape),
+                in1=ab[:, 1, g, :, :].unsqueeze(2).to_broadcast(shape),
                 op=mybir.AluOpType.mult,
             )
 
-        def quantise(m, g0):
+        def quantise(g, i):
+            columns = slice(i.start * N2, i.stop * N2)
             nc.vector.quantize_mx(
-                out=codes[m][:, g0 : g0 + GROUP, :].rearrange("p g c -> p (g c)").bitcast(FP8X4),
-                scales=code_scales[m][:, g0 : g0 + GROUP, :].rearrange("p g c -> p (g c)"),
-                in_=prod[m][:, g0 : g0 + GROUP, :, :, :].rearrange("p g i j t -> p (g i j t)"),
+                out=codes[:, g, columns].rearrange("p g c -> p (g c)").bitcast(FP8X4),
+                scales=code_scales[:, g, columns].rearrange("p g c -> p (g c)"),
+                in_=prod[:, g, i, :, :].rearrange("p g i j t -> p (g i j t)"),
             )
 
-        def contract(m, g0):
-            for g in range(g0, g0 + GROUP):
-                nc.tensor.matmul_mx(
-                    out=acc[m][:],
-                    lhsT=codes[m][:, g, :].bitcast(FP8X4),
-                    lhsT_scale=code_scales[m][:, g, :],
-                    rhs=w_words[:, g, :].bitcast(FP4X4),
-                    rhs_scale=w_scales[:, g, :],
-                    start=(g == 0),
-                    stop=(g == PASSES - 1),
-                )
+        def contract(gs, i):
+            for g in range(gs.start, gs.stop):
+                for m in range(i.start // I_TILE, i.stop // I_TILE):
+                    columns = slice(m * P, (m + 1) * P)
+                    nc.tensor.matmul_mx(
+                        out=acc[m][:],
+                        lhsT=codes[:, g, columns].bitcast(FP8X4),
+                        lhsT_scale=code_scales[:, g, columns],
+                        rhs=w_words[:, g, :].bitcast(FP4X4),
+                        rhs_scale=w_scales[:, g, :],
+                        start=(g == 0),
+                        stop=(g == PASSES - 1),
+                    )
 
         def finish(m):
             result = keep.tile([P, N3], F32, name="result%d" % m)
             nc.vector.tensor_tensor(
-                out=result[:], in0=acc[m][:], in1=x_sb[m][:], op=mybir.AluOpType.subtract
+                out=result[:], in0=acc[m][:], in1=x_sb[:, m, :], op=mybir.AluOpType.subtract
             )
-            nc.sync.dma_start(out=out[:, m * J_TILE : (m + 1) * J_TILE, :], in_=result[:])
+            nc.sync.dma_start(out=out[m * I_TILE : (m + 1) * I_TILE, :, :], in_=result[:])
 
-        steps = [(m, g0) for m in range(M_TILES) for g0 in range(0, PASSES, GROUP)]
+        both = slice(0, N1)
+        steps = [(slice(g, g + 2), both) for g in range(0, PASSES - 2, 2)]
+        for m in range(M_TILES):
+            for g in range(PASSES - 2, PASSES):
+                steps.append((slice(g, g + 1), slice(m * I_TILE, (m + 1) * I_TILE)))
         for s in range(len(steps) + 1):
             if s < len(steps):
                 multiply(*steps[s])

@@ -39,8 +39,8 @@ def tile_recon_loss_pa_kernel(tc, X, A, B, C_words, C_scales, out):
             tile = keep.tile([P, K_PASS], BF16, name="raw%d" % c)
             columns = slice(c * CHUNK * K_PASS, (c + 1) * CHUNK * K_PASS)
             half = P // 2
-            nc.sync.dma_start(out=tile[0:half, :], in_=A[:, columns].rearrange("i (g r) -> g i r", r=K_PASS))
-            nc.scalar.dma_start(out=tile[half:P, :], in_=B[:, columns].rearrange("j (g r) -> g j r", r=K_PASS))
+            nc.sync.dma_start(out=tile[0:half, :], in_=A[:, columns].rearrange("i (g r) -> i g r", r=K_PASS))
+            nc.scalar.dma_start(out=tile[half:P, :], in_=B[:, columns].rearrange("j (g r) -> j g r", r=K_PASS))
             raw.append(tile)
 
         ident = keep.tile([P, P], F32, name="ident")
@@ -69,13 +69,13 @@ def tile_recon_loss_pa_kernel(tc, X, A, B, C_words, C_scales, out):
             turned = psum.tile([P, 2, P], F32, name="turned%d" % c)
             for u in range(2):
                 nc.tensor.transpose(turned[:, u, :], words[:, u : K_PASS // 2 : 2], ident[:])
-            target = ab[:, :, c * CHUNK : (c + 1) * CHUNK, :, :].rearrange("p f g i t -> p f (g i t)").bitcast(F32)
-            target = target.rearrange("p f (q u) -> p f q u", u=2)
-            source = turned[:].rearrange("p u (f q) -> p f q u", f=2)
-            if c == 0:
-                nc.vector.tensor_copy(out=target, in_=source)
-            else:
-                nc.scalar.copy(out=target, in_=source)
+            source = turned[:].rearrange("p u (f row g) -> p f g row u", f=2, g=CHUNK)
+            for f in range(2):
+                target = ab[:, f, c * CHUNK : (c + 1) * CHUNK, :, :].bitcast(F32)
+                if c == 0 and f == 0:
+                    nc.vector.tensor_copy(out=target, in_=source[:, f, :, :, :])
+                else:
+                    nc.scalar.copy(out=target, in_=source[:, f, :, :, :])
 
         prod = keep.tile([P, PASSES, N1, N2, PACK], BF16, name="prod", align_bytes=64)
         codes = keep.tile([P, PASSES, N1 * N2], U32, name="codes", align_bytes=64)
@@ -118,7 +118,7 @@ def tile_recon_loss_pa_kernel(tc, X, A, B, C_words, C_scales, out):
             nc.vector.tensor_tensor(
                 out=result[:], in0=acc[m][:], in1=x_sb[:, m, :], op=mybir.AluOpType.subtract
             )
-            nc.sync.dma_start(out=out[m * I_TILE : (m + 1) * I_TILE, :, :], in_=result[:])
+            nc.sync.dma_start(out=out[m * I_TILE : (m + 1) * I_TILE, :, :].rearrange("i j n -> (i j) n"), in_=result[:])
 
         both = slice(0, N1)
         steps = [(slice(g, g + 2), both) for g in range(0, PASSES - 2, 2)]

@@ -72,7 +72,7 @@ def tile_recon_loss_pa_kernel(tc, X, A, B, C_words, C_scales, out):
             source = turned[:].rearrange("p u (f row g) -> p f g row u", f=2, g=CHUNK)
             for f in range(2):
                 target = ab[:, f, c * CHUNK : (c + 1) * CHUNK, :, :].bitcast(F32)
-                if c == 0 and f == 0:
+                if c == 0:
                     nc.vector.tensor_copy(out=target, in_=source[:, f, :, :, :])
                 else:
                     nc.scalar.copy(out=target, in_=source[:, f, :, :, :])
@@ -114,17 +114,21 @@ def tile_recon_loss_pa_kernel(tc, X, A, B, C_words, C_scales, out):
                     )
 
         def finish(m):
-            result = keep.tile([P, N3], F32, name="result%d" % m)
-            nc.vector.tensor_tensor(
-                out=result[:], in0=acc[m][:], in1=x_sb[:, m, :], op=mybir.AluOpType.subtract
-            )
-            nc.sync.dma_start(out=out[m * I_TILE : (m + 1) * I_TILE, :, :].rearrange("i j n -> (i j) n"), in_=result[:])
+            rows = out[m * I_TILE : (m + 1) * I_TILE, :, :].rearrange("i j n -> (i j) n")
+            width = N3 // 2 if m == M_TILES - 1 else N3
+            for n0 in range(0, N3, width):
+                columns = slice(n0, n0 + width)
+                result = keep.tile([P, width], F32, name="result%d_%d" % (m, n0))
+                nc.vector.tensor_tensor(
+                    out=result[:], in0=acc[m][:, columns], in1=x_sb[:, m, columns], op=mybir.AluOpType.subtract
+                )
+                nc.sync.dma_start(out=rows[:, columns], in_=result[:])
 
         both = slice(0, N1)
-        steps = [(slice(g, g + 2), both) for g in range(0, PASSES - 2, 2)]
+        steps = [(slice(g, g + 2), both) for g in range(0, PASSES - 4, 2)]
+        steps += [(slice(g, g + 1), both) for g in range(PASSES - 4, PASSES - 2)]
         for m in range(M_TILES):
-            for g in range(PASSES - 2, PASSES):
-                steps.append((slice(g, g + 1), slice(m * I_TILE, (m + 1) * I_TILE)))
+            steps += [(slice(g, g + 1), slice(m * I_TILE, (m + 1) * I_TILE)) for g in range(PASSES - 2, PASSES)]
         for s in range(len(steps) + 1):
             if s < len(steps):
                 multiply(*steps[s])

@@ -22,6 +22,8 @@ CHUNKS = PASSES // CHUNK
 I_TILE = P // N2
 M_TILES = N1 // I_TILE
 LOAD_PASSES = 4
+SCALAR_PASSES = range(14, 16)
+LAST_PASS = SCALAR_PASSES.start - 1
 QUADRANTS = 4
 
 FLOPS = 2 * N1 * N2 * N3 * R
@@ -77,10 +79,24 @@ def tile_recon_loss_pa_kernel(tc, X, A, B, C_words, C_scales, out):
                 else:
                     nc.scalar.copy(out=target, in_=source[:, f, :, :, :])
 
+        a_scale = keep.tile([P, len(SCALAR_PASSES), N1, PACK], F32, name="a_scale")
+        nc.scalar.copy(out=a_scale[:], in_=ab[:, 0, SCALAR_PASSES.start : SCALAR_PASSES.stop, :, :])
+
         prod = keep.tile([P, PASSES, N1, N2, PACK], BF16, name="prod", align_bytes=64)
         codes = keep.tile([P, PASSES, N1 * N2], U32, name="codes", align_bytes=64)
         code_scales = keep.tile([P, PASSES, N1 * N2], U8, name="code_scales", align_bytes=64)
         acc = [psum.tile([P, N3], F32, name="acc%d" % m) for m in range(M_TILES)]
+
+        for m in range(M_TILES):
+            for k, g in enumerate(SCALAR_PASSES):
+                for i in range(m * I_TILE, (m + 1) * I_TILE):
+                    for t in range(PACK):
+                        nc.scalar.activation(
+                            out=prod[:, g, i, :, t],
+                            in_=ab[:, 1, g, :, t],
+                            func=mybir.ActivationFunctionType.Copy,
+                            scale=a_scale[:, k, i, t : t + 1],
+                        )
 
         def multiply(g, i):
             shape = [P, g.stop - g.start, i.stop - i.start, N2, PACK]
@@ -110,7 +126,7 @@ def tile_recon_loss_pa_kernel(tc, X, A, B, C_words, C_scales, out):
                         rhs=w_words[:, g, :].bitcast(FP4X4),
                         rhs_scale=w_scales[:, g, :],
                         start=(g == 0),
-                        stop=(g == PASSES - 1),
+                        stop=(g == LAST_PASS),
                     )
 
         def finish(m):
@@ -125,12 +141,13 @@ def tile_recon_loss_pa_kernel(tc, X, A, B, C_words, C_scales, out):
                 nc.sync.dma_start(out=rows[:, columns], in_=result[:])
 
         both = slice(0, N1)
-        steps = [(slice(g, g + 2), both) for g in range(0, PASSES - 4, 2)]
-        steps += [(slice(g, g + 1), both) for g in range(PASSES - 4, PASSES - 2)]
+        steps = [(slice(g, g + 2), both) for g in range(0, LAST_PASS - 1, 2)]
+        steps += [(slice(LAST_PASS - 1, LAST_PASS), both)]
         for m in range(M_TILES):
-            steps += [(slice(g, g + 1), slice(m * I_TILE, (m + 1) * I_TILE)) for g in range(PASSES - 2, PASSES)]
+            tile = slice(m * I_TILE, (m + 1) * I_TILE)
+            steps += [(slice(g, g + 1), tile) for g in (*SCALAR_PASSES, LAST_PASS)]
         for s in range(len(steps) + 1):
-            if s < len(steps):
+            if s < len(steps) and steps[s][0].start not in SCALAR_PASSES:
                 multiply(*steps[s])
             if s >= 1:
                 quantise(*steps[s - 1])

@@ -141,11 +141,25 @@ def tile_recon_loss_pa_kernel(tc, X, A, B, C_words, C_scales, out):
                 nc.sync.dma_start(out=rows[:, columns], in_=result[:])
 
         both = slice(0, N1)
-        steps = [(slice(g, g + 2), both) for g in range(0, LAST_PASS - 1, 2)]
-        steps += [(slice(LAST_PASS - 1, LAST_PASS), both)]
-        for m in range(M_TILES):
-            tile = slice(m * I_TILE, (m + 1) * I_TILE)
-            steps += [(slice(g, g + 1), tile) for g in (*SCALAR_PASSES, LAST_PASS)]
+        tiles = [slice(m * I_TILE, (m + 1) * I_TILE) for m in range(M_TILES)]
+
+        def step(g, i):
+            return (slice(g, g + 1), i)
+
+        s0, s1 = SCALAR_PASSES
+        steps = [(slice(g, g + 2), both) for g in range(0, LAST_PASS - 5, 2)]
+        steps += [
+            step(s0, tiles[0]),
+            step(s1, tiles[0]),
+            (slice(LAST_PASS - 5, LAST_PASS - 3), both),
+            step(LAST_PASS - 3, both),
+            step(s0, tiles[1]),
+            step(LAST_PASS - 2, both),
+            step(LAST_PASS - 1, both),
+            step(LAST_PASS, tiles[0]),
+            step(s1, tiles[1]),
+            step(LAST_PASS, tiles[1]),
+        ]
         for s in range(len(steps) + 1):
             if s < len(steps) and steps[s][0].start not in SCALAR_PASSES:
                 multiply(*steps[s])

@@ -21,9 +21,9 @@ CHUNK = P // ROWS
 CHUNKS = PASSES // CHUNK
 I_TILE = P // N2
 M_TILES = N1 // I_TILE
-LOAD_PASSES = 4
-SCALAR_PASSES = range(14, 16)
-LAST_PASS = SCALAR_PASSES.start - 1
+SCALAR_PASSES = range(2, 4)
+LAST_PASS = PASSES - 1
+W_LOADS = [range(0, 2), range(4, 8), range(8, 12), range(12, 16), SCALAR_PASSES]
 QUADRANTS = 4
 
 FLOPS = 2 * N1 * N2 * N3 * R
@@ -36,14 +36,16 @@ def tile_recon_loss_pa_kernel(tc, X, A, B, C_words, C_scales, out):
         psum = ctx.enter_context(tc.psum_pool(name="psum", bufs=1))
         ctx.enter_context(tc.manual_schedule())
 
-        raw = []
-        for c in range(CHUNKS):
-            tile = keep.tile([P, K_PASS], BF16, name="raw%d" % c)
+        raw = [keep.tile([P, K_PASS], BF16, name="raw%d" % c) for c in range(CHUNKS)]
+
+        def load_chunk(c, a_queue, b_queue):
             columns = slice(c * CHUNK * K_PASS, (c + 1) * CHUNK * K_PASS)
             half = P // 2
-            nc.sync.dma_start(out=tile[0:half, :], in_=A[:, columns].rearrange("i (g r) -> i g r", r=K_PASS))
-            nc.scalar.dma_start(out=tile[half:P, :], in_=B[:, columns].rearrange("j (g r) -> j g r", r=K_PASS))
-            raw.append(tile)
+            a_queue.dma_start(out=raw[c][0:half, :], in_=A[:, columns].rearrange("i (g r) -> i g r", r=K_PASS))
+            b_queue.dma_start(out=raw[c][half:P, :], in_=B[:, columns].rearrange("j (g r) -> j g r", r=K_PASS))
+
+        for c in range(2):
+            load_chunk(c, nc.sync, nc.scalar)
 
         ident = keep.tile([P, P], F32, name="ident")
         make_identity(nc, ident[:])
@@ -52,21 +54,28 @@ def tile_recon_loss_pa_kernel(tc, X, A, B, C_words, C_scales, out):
         scale_rows = C_scales.bitcast(I32)
         w_words = keep.tile([P, PASSES, 2 * N3], U8, name="w_words", align_bytes=64)
         word_rows = C_words.bitcast(I32).rearrange("g p w -> p g w")
-        for g0 in range(0, PASSES, LOAD_PASSES):
-            group = slice(g0, g0 + LOAD_PASSES)
+        def load_scales(group, quad):
+            nc.sync.dma_start(
+                out=w_scales[32 * quad : 32 * quad + 4, group, :].bitcast(I32),
+                in_=scale_rows[group, 4 * quad : 4 * quad + 4, :].rearrange("g q n -> q g n"),
+            )
+
+        for k, passes in enumerate(W_LOADS):
+            group = slice(passes.start, passes.stop)
             nc.vector.memset(w_scales[:, group, :].bitcast(I32), 0)
-            for quad in range(QUADRANTS):
-                nc.sync.dma_start(
-                    out=w_scales[32 * quad : 32 * quad + 4, group, :].bitcast(I32),
-                    in_=scale_rows[group, 4 * quad : 4 * quad + 4, :].rearrange("g q n -> q g n"),
-                )
+            for quad in range(QUADRANTS - 1):
+                load_scales(group, quad)
             nc.sync.dma_start(out=w_words[:, group, :].bitcast(I32), in_=word_rows[:, group, :])
+            load_scales(group, QUADRANTS - 1)
+            if k + 2 < CHUNKS:
+                load_chunk(k + 2, nc.sync, nc.sync)
 
         x_sb = keep.tile([P, M_TILES, N3], BF16, name="x_sb")
         nc.sync.dma_start(out=x_sb[:], in_=X.rearrange("(m i) j n -> (i j) m n", m=M_TILES))
 
         ab = keep.tile([P, 2, PASSES, N1, PACK], BF16, name="ab")
-        for c in range(CHUNKS):
+
+        def turn(c, copy):
             words = raw[c][:].bitcast(F32)
             turned = psum.tile([P, 2, P], F32, name="turned%d" % c)
             for u in range(2):
@@ -74,29 +83,28 @@ def tile_recon_loss_pa_kernel(tc, X, A, B, C_words, C_scales, out):
             source = turned[:].rearrange("p u (f row g) -> p f g row u", f=2, g=CHUNK)
             for f in range(2):
                 target = ab[:, f, c * CHUNK : (c + 1) * CHUNK, :, :].bitcast(F32)
-                if c == 0:
-                    nc.vector.tensor_copy(out=target, in_=source[:, f, :, :, :])
-                else:
-                    nc.scalar.copy(out=target, in_=source[:, f, :, :, :])
+                copy(out=target, in_=source[:, f, :, :, :])
+
+        turn(0, nc.vector.tensor_copy)
 
         a_scale = keep.tile([P, len(SCALAR_PASSES), N1, PACK], F32, name="a_scale")
         nc.scalar.copy(out=a_scale[:], in_=ab[:, 0, SCALAR_PASSES.start : SCALAR_PASSES.stop, :, :])
+        turn(1, nc.scalar.copy)
 
         prod = keep.tile([P, PASSES, N1, N2, PACK], BF16, name="prod", align_bytes=64)
         codes = keep.tile([P, PASSES, N1 * N2], U32, name="codes", align_bytes=64)
         code_scales = keep.tile([P, PASSES, N1 * N2], U8, name="code_scales", align_bytes=64)
         acc = [psum.tile([P, N3], F32, name="acc%d" % m) for m in range(M_TILES)]
 
-        for m in range(M_TILES):
-            for k, g in enumerate(SCALAR_PASSES):
-                for i in range(m * I_TILE, (m + 1) * I_TILE):
-                    for t in range(PACK):
-                        nc.scalar.activation(
-                            out=prod[:, g, i, :, t],
-                            in_=ab[:, 1, g, :, t],
-                            func=mybir.ActivationFunctionType.Copy,
-                            scale=a_scale[:, k, i, t : t + 1],
-                        )
+        def scalar_products(g, m):
+            for i in range(m * I_TILE, (m + 1) * I_TILE):
+                for t in range(PACK):
+                    nc.scalar.activation(
+                        out=prod[:, g, i, :, t],
+                        in_=ab[:, 1, g, :, t],
+                        func=mybir.ActivationFunctionType.Copy,
+                        scale=a_scale[:, g - SCALAR_PASSES.start, i, t : t + 1],
+                    )
 
         def multiply(g, i):
             shape = [P, g.stop - g.start, i.stop - i.start, N2, PACK]
@@ -147,11 +155,12 @@ def tile_recon_loss_pa_kernel(tc, X, A, B, C_words, C_scales, out):
             return (slice(g, g + 1), i)
 
         s0, s1 = SCALAR_PASSES
-        steps = [(slice(g, g + 2), both) for g in range(0, LAST_PASS - 5, 2)]
+        pairs = [(slice(g, g + 2), both) for g in (0, 4, 6, 8, 10)]
+        steps = [step(0, both), step(1, both)] + pairs[1:4]
         steps += [
             step(s0, tiles[0]),
             step(s1, tiles[0]),
-            (slice(LAST_PASS - 5, LAST_PASS - 3), both),
+            pairs[4],
             step(LAST_PASS - 3, both),
             step(s0, tiles[1]),
             step(LAST_PASS - 2, both),
@@ -160,11 +169,18 @@ def tile_recon_loss_pa_kernel(tc, X, A, B, C_words, C_scales, out):
             step(s1, tiles[1]),
             step(LAST_PASS, tiles[1]),
         ]
+        scalar_products(s0, 0)
+        turn(2, nc.scalar.copy)
+        scalar_products(s1, 0)
         for s in range(len(steps) + 1):
             if s < len(steps) and steps[s][0].start not in SCALAR_PASSES:
                 multiply(*steps[s])
             if s >= 1:
                 quantise(*steps[s - 1])
                 contract(*steps[s - 1])
+            if s == 3:
+                turn(3, nc.scalar.copy)
+                scalar_products(s0, 1)
+                scalar_products(s1, 1)
         for m in range(M_TILES):
             finish(m)

@@ -62,7 +62,8 @@ def tile_recon_loss_pa_kernel(tc, X, A, B, C_words, C_scales, out):
 
         for k, passes in enumerate(W_LOADS):
             group = slice(passes.start, passes.stop)
-            nc.vector.memset(w_scales[:, group, :].bitcast(I32), 0)
+            zeroing = nc.vector if k == 0 else nc.gpsimd
+            zeroing.memset(w_scales[:, group, :].bitcast(I32), 0)
             for quad in range(QUADRANTS - 1):
                 load_scales(group, quad)
             nc.sync.dma_start(out=w_words[:, group, :].bitcast(I32), in_=word_rows[:, group, :])
@@ -75,21 +76,23 @@ def tile_recon_loss_pa_kernel(tc, X, A, B, C_words, C_scales, out):
 
         ab = keep.tile([P, 2, PASSES, N1, PACK], BF16, name="ab")
 
-        def turn(c, copy):
+        def turn(c, copies):
             words = raw[c][:].bitcast(F32)
             turned = psum.tile([P, 2, P], F32, name="turned%d" % c)
             for u in range(2):
                 nc.tensor.transpose(turned[:, u, :], words[:, u : K_PASS // 2 : 2], ident[:])
             source = turned[:].rearrange("p u (f row g) -> p f g row u", f=2, g=CHUNK)
-            for f in range(2):
-                target = ab[:, f, c * CHUNK : (c + 1) * CHUNK, :, :].bitcast(F32)
-                copy(out=target, in_=source[:, f, :, :, :])
+            for copy, g0, g1 in copies:
+                for f in range(2):
+                    target = ab[:, f, c * CHUNK + g0 : c * CHUNK + g1, :, :].bitcast(F32)
+                    copy(out=target, in_=source[:, f, g0:g1, :, :])
 
-        turn(0, nc.vector.tensor_copy)
+        whole = [(nc.scalar.copy, 0, CHUNK)]
+        turn(0, [(nc.vector.tensor_copy, 0, 1), (nc.vector.tensor_copy, 1, CHUNK)])
 
         a_scale = keep.tile([P, len(SCALAR_PASSES), N1, PACK], F32, name="a_scale")
         nc.scalar.copy(out=a_scale[:], in_=ab[:, 0, SCALAR_PASSES.start : SCALAR_PASSES.stop, :, :])
-        turn(1, nc.scalar.copy)
+        turn(1, whole)
 
         prod = keep.tile([P, PASSES, N1, N2, PACK], BF16, name="prod", align_bytes=64)
         codes = keep.tile([P, PASSES, N1 * N2], U32, name="codes", align_bytes=64)
@@ -164,13 +167,14 @@ def tile_recon_loss_pa_kernel(tc, X, A, B, C_words, C_scales, out):
             step(LAST_PASS - 3, both),
             step(s0, tiles[1]),
             step(LAST_PASS - 2, both),
-            step(LAST_PASS - 1, both),
+            step(LAST_PASS - 1, tiles[0]),
             step(LAST_PASS, tiles[0]),
+            step(LAST_PASS - 1, tiles[1]),
             step(s1, tiles[1]),
             step(LAST_PASS, tiles[1]),
         ]
         scalar_products(s0, 0)
-        turn(2, nc.scalar.copy)
+        turn(2, whole)
         scalar_products(s1, 0)
         for s in range(len(steps) + 1):
             if s < len(steps) and steps[s][0].start not in SCALAR_PASSES:
@@ -179,7 +183,7 @@ def tile_recon_loss_pa_kernel(tc, X, A, B, C_words, C_scales, out):
                 quantise(*steps[s - 1])
                 contract(*steps[s - 1])
             if s == 3:
-                turn(3, nc.scalar.copy)
+                turn(3, whole)
                 scalar_products(s0, 1)
                 scalar_products(s1, 1)
         for m in range(M_TILES):

from contextlib import ExitStack

import concourse.mybir as mybir
from concourse.masks import make_identity

F32 = mybir.dt.float32
BF16 = mybir.dt.bfloat16
U8 = mybir.dt.uint8
U32 = mybir.dt.uint32
I32 = mybir.dt.int32
FP8X4 = mybir.dt.float8_e4m3fn_x4
FP4X4 = mybir.dt.float4_e2m1fn_x4

N1, N2, N3, R = 16, 16, 512, 8192
P = 128
PACK = 4
K_PASS = P * PACK
PASSES = R // K_PASS
ROWS = N1 + N2
CHUNK = P // ROWS
CHUNKS = PASSES // CHUNK
I_TILE = P // N2
M_TILES = N1 // I_TILE
SCALAR_PASSES = range(2, 4)
LAST_PASS = PASSES - 1
W_LOADS = [range(0, 2), range(4, 8), range(8, 12), range(12, 16), SCALAR_PASSES]
QUADRANTS = 4

FLOPS = 2 * N1 * N2 * N3 * R


def tile_recon_loss_pa_kernel(tc, X, A, B, C_words, C_scales, out):
    nc = tc.nc
    with ExitStack() as ctx:
        keep = ctx.enter_context(tc.tile_pool(name="keep", bufs=1))
        psum = ctx.enter_context(tc.psum_pool(name="psum", bufs=1))
        ctx.enter_context(tc.manual_schedule())

        raw = [keep.tile([P, K_PASS], BF16, name="raw%d" % c) for c in range(CHUNKS)]

        def load_chunk(c, a_queue, b_queue):
            columns = slice(c * CHUNK * K_PASS, (c + 1) * CHUNK * K_PASS)
            half = P // 2
            a_queue.dma_start(out=raw[c][0:half, :], in_=A[:, columns].rearrange("i (g r) -> i g r", r=K_PASS))
            b_queue.dma_start(out=raw[c][half:P, :], in_=B[:, columns].rearrange("j (g r) -> j g r", r=K_PASS))

        for c in range(2):
            load_chunk(c, nc.sync, nc.scalar)

        ident = keep.tile([P, P], F32, name="ident")
        make_identity(nc, ident[:])

        w_scales = keep.tile([P, PASSES, N3], U8, name="w_scales", align_bytes=64)
        scale_rows = C_scales.bitcast(I32)
        w_words = keep.tile([P, PASSES, 2 * N3], U8, name="w_words", align_bytes=64)
        word_rows = C_words.bitcast(I32).rearrange("g p w -> p g w")
        def load_scales(group, quad):
            nc.sync.dma_start(
                out=w_scales[32 * quad : 32 * quad + 4, group, :].bitcast(I32),
                in_=scale_rows[group, 4 * quad : 4 * quad + 4, :].rearrange("g q n -> q g n"),
            )

        for k, passes in enumerate(W_LOADS):
            group = slice(passes.start, passes.stop)
            zeroing = nc.vector if k == 0 else nc.gpsimd
            zeroing.memset(w_scales[:, group, :].bitcast(I32), 0)
            for quad in range(QUADRANTS - 1):
                load_scales(group, quad)
            nc.sync.dma_start(out=w_words[:, group, :].bitcast(I32), in_=word_rows[:, group, :])
            load_scales(group, QUADRANTS - 1)
            if k + 2 < CHUNKS:
                load_chunk(k + 2, nc.sync, nc.sync)

        x_sb = keep.tile([P, M_TILES, N3], BF16, name="x_sb")
        nc.sync.dma_start(out=x_sb[:], in_=X.rearrange("(m i) j n -> (i j) m n", m=M_TILES))

        ab = keep.tile([P, 2, PASSES, N1, PACK], BF16, name="ab")

        def turn(c, copies):
            words = raw[c][:].bitcast(F32)
            turned = psum.tile([P, 2, P], F32, name="turned%d" % c)
            for u in range(2):
                nc.tensor.transpose(turned[:, u, :], words[:, u : K_PASS // 2 : 2], ident[:])
            source = turned[:].rearrange("p u (f row g) -> p f g row u", f=2, g=CHUNK)
            for copy, g0, g1 in copies:
                for f in range(2):
                    target = ab[:, f, c * CHUNK + g0 : c * CHUNK + g1, :, :].bitcast(F32)
                    copy(out=target, in_=source[:, f, g0:g1, :, :])

        whole = [(nc.scalar.copy, 0, CHUNK)]
        turn(0, [(nc.vector.tensor_copy, 0, 1), (nc.vector.tensor_copy, 1, CHUNK)])

        a_scale = keep.tile([P, len(SCALAR_PASSES), N1, PACK], F32, name="a_scale")
        nc.scalar.copy(out=a_scale[:], in_=ab[:, 0, SCALAR_PASSES.start : SCALAR_PASSES.stop, :, :])
        turn(1, whole)

        prod = keep.tile([P, PASSES, N1, N2, PACK], BF16, name="prod", align_bytes=64)
        codes = keep.tile([P, PASSES, N1 * N2], U32, name="codes", align_bytes=64)
        code_scales = keep.tile([P, PASSES, N1 * N2], U8, name="code_scales", align_bytes=64)
        acc = [psum.tile([P, N3], F32, name="acc%d" % m) for m in range(M_TILES)]

        def scalar_products(g, m):
            for i in range(m * I_TILE, (m + 1) * I_TILE):
                for t in range(PACK):
                    nc.scalar.activation(
                        out=prod[:, g, i, :, t],
                        in_=ab[:, 1, g, :, t],
                        func=mybir.ActivationFunctionType.Copy,
                        scale=a_scale[:, g - SCALAR_PASSES.start, i, t : t + 1],
                    )

        def multiply(g, i):
            shape = [P, g.stop - g.start, i.stop - i.start, N2, PACK]
            nc.vector.tensor_tensor(
                out=prod[:, g, i, :, :],
                in0=ab[:, 0, g, i, :].unsqueeze(3).to_broadcast(shape),
                in1=ab[:, 1, g, :, :].unsqueeze(2).to_broadcast(shape),
                op=mybir.AluOpType.mult,
            )

        def quantise(g, i):
            columns = slice(i.start * N2, i.stop * N2)
            nc.vector.quantize_mx(
                out=codes[:, g, columns].rearrange("p g c -> p (g c)").bitcast(FP8X4),
                scales=code_scales[:, g, columns].rearrange("p g c -> p (g c)"),
                in_=prod[:, g, i, :, :].rearrange("p g i j t -> p (g i j t)"),
            )

        def contract(gs, i):
            for g in range(gs.start, gs.stop):
                for m in range(i.start // I_TILE, i.stop // I_TILE):
                    columns = slice(m * P, (m + 1) * P)
                    nc.tensor.matmul_mx(
                        out=acc[m][:],
                        lhsT=codes[:, g, columns].bitcast(FP8X4),
                        lhsT_scale=code_scales[:, g, columns],
                        rhs=w_words[:, g, :].bitcast(FP4X4),
                        rhs_scale=w_scales[:, g, :],
                        start=(g == 0),
                        stop=(g == LAST_PASS),
                    )

        def finish(m):
            rows = out[m * I_TILE : (m + 1) * I_TILE, :, :].rearrange("i j n -> (i j) n")
            width = N3 // 2 if m == M_TILES - 1 else N3
            for n0 in range(0, N3, width):
                columns = slice(n0, n0 + width)
                result = keep.tile([P, width], F32, name="result%d_%d" % (m, n0))
                nc.vector.tensor_tensor(
                    out=result[:], in0=acc[m][:, columns], in1=x_sb[:, m, columns], op=mybir.AluOpType.subtract
                )
                nc.sync.dma_start(out=rows[:, columns], in_=result[:])

        both = slice(0, N1)
        tiles = [slice(m * I_TILE, (m + 1) * I_TILE) for m in range(M_TILES)]

        def step(g, i):
            return (slice(g, g + 1), i)

        s0, s1 = SCALAR_PASSES
        pairs = [(slice(g, g + 2), both) for g in (0, 4, 6, 8, 10)]
        steps = [step(0, both), step(1, both)] + pairs[1:4]
        steps += [
            step(s0, tiles[0]),
            step(s1, tiles[0]),
            pairs[4],
            step(LAST_PASS - 3, both),
            step(s0, tiles[1]),
            step(LAST_PASS - 2, both),
            step(LAST_PASS - 1, tiles[0]),
            step(LAST_PASS, tiles[0]),
            step(LAST_PASS - 1, tiles[1]),
            step(s1, tiles[1]),
            step(LAST_PASS, tiles[1]),
        ]
        scalar_products(s0, 0)
        turn(2, whole)
        scalar_products(s1, 0)
        for s in range(len(steps) + 1):
            if s < len(steps) and steps[s][0].start not in SCALAR_PASSES:
                multiply(*steps[s])
            if s >= 1:
                quantise(*steps[s - 1])
                contract(*steps[s - 1])
            if s == 3:
                turn(3, whole)
                scalar_products(s0, 1)
                scalar_products(s1, 1)
        for m in range(M_TILES):
            finish(m)
